import numpy as np
import ml_dtypes


def mxq(x, axis, fmt="e4m3"):
    dtype, down = {"e4m3": (ml_dtypes.float8_e4m3fn, 7), "e5m2": (ml_dtypes.float8_e5m2, 14)}[fmt]
    v = np.moveaxis(np.asarray(x, np.float32).astype(ml_dtypes.bfloat16).astype(np.float64), axis, -1)
    blocks = v.reshape(v.shape[:-1] + (-1, 32))
    amax = np.abs(blocks).max(-1, keepdims=True)
    byte = np.maximum(np.where(amax > 0, np.frexp(amax)[1] - 1 + 127, 0) - down, 1)
    scale = np.exp2(byte - 127.0)
    codes = (blocks / scale).astype(np.float32).astype(dtype).astype(np.float64)
    return np.moveaxis((codes * scale).reshape(v.shape), -1, axis)


WIDE = False


def mx_kscale(k):
    if not WIDE:
        return np.ones(k)
    levels = np.array([10, -10, 5, -5, 0])
    if k % 512:
        return np.exp2(np.random.permutation(np.resize(levels, k // 32))).repeat(32)
    a = np.empty((k // 512, 16))
    for p in range(k // 512):
        a[p, :8] = np.random.permutation(np.resize(levels, 8))
        for g in range(8):
            far = levels[np.abs(levels - a[p, g]) >= 10]
            a[p, g + 8] = far[np.random.randint(len(far))]
    return np.exp2(a.ravel()).repeat(32)


BF16 = ml_dtypes.bfloat16


def bf(x):
    return np.asarray(x, np.float32).astype(BF16)


def f64(x):
    return np.asarray(x).astype(np.float64)


B, S, D, DR = 8, 512, 1024, 512
G = 1.4 * (D / DR) ** 0.25 / np.sqrt(D)


def setup_inputs():
    s = mx_kscale(D)
    t = mx_kscale(DR)
    mask = (np.random.random((S, S)) < 0.5) & ~np.eye(S, dtype=bool)
    return {"q_lin": bf(np.random.standard_normal((B, S, D)) * s),
            "k_lin": bf(np.random.standard_normal((B, S, D)) * s),
            "rotation_params": bf(np.random.standard_normal((DR, D)) * G * t[:, None] / s),
            "entangle_params": bf(np.random.standard_normal((DR, D)) * G / t[:, None] / s),
            "mask": mask}


def reference(q_lin, k_lin, rotation_params, entangle_params, mask):
    q = mxq(f64(q_lin), 2, "e4m3") @ mxq(f64(rotation_params), 1, "e4m3").T
    k = mxq(f64(k_lin), 2, "e4m3") @ mxq(f64(entangle_params), 1, "e4m3").T
    scores = (mxq(q, 2, "e4m3") @ mxq(k, 2, "e4m3").transpose(0, 2, 1)) / np.sqrt(D)
    scores = np.where(f64(mask) > 0.5, -np.inf, scores)
    e = np.exp(scores - scores.max(-1, keepdims=True))
    return e / e.sum(-1, keepdims=True)

@@ -1,0 +1,281 @@
+from contextlib import ExitStack
+
+import concourse.mybir as mybir
+from concourse.masks import make_identity
+
+F32 = mybir.dt.float32
+BF16 = mybir.dt.bfloat16
+I32 = mybir.dt.int32
+U32 = mybir.dt.uint32
+U8 = mybir.dt.uint8
+FP8X4 = mybir.dt.float8_e4m3fn_x4
+ALU = mybir.AluOpType
+ACT = mybir.ActivationFunctionType
+
+P = 128
+PACK = 4
+K_PASS = P * PACK
+BANK = 512
+PSUM_BANKS = 8
+
+BATCH = 8
+TOKENS = 512
+WIDTH = 1024
+FEATURES = 512
+CHUNKS = TOKENS // P
+PASSES = WIDTH // K_PASS
+ROW_WORDS = WIDTH // 2
+PASS_WORDS = K_PASS // 2
+UNITS = 2 * BATCH
+PAIR = 2
+PAIRS = BATCH * CHUNKS // PAIR
+PREFETCH = 4
+UNIT_BANKS = PASSES * CHUNKS // 2
+VECTOR_EVERY = 3
+
+SCORE_SCALE = 1.0 / 32.0
+CAP = 1.0e38
+
+FLOPS = 2 * (2 * BATCH * TOKENS * WIDTH * FEATURES) + 2 * BATCH * TOKENS * TOKENS * FEATURES
+
+
+def tile_selfattention_pa_t_kernel(
+    tc, q_lin, k_lin, rotation_params, entangle_params, mask, out
+):
+    nc = tc.nc
+    with ExitStack() as ctx:
+        const = ctx.enter_context(tc.tile_pool(name="const", bufs=1))
+        rows_pool = ctx.enter_context(tc.tile_pool(name="rows", bufs=PREFETCH + 2))
+        grouped_pool = ctx.enter_context(tc.tile_pool(name="grouped", bufs=2))
+        unit_mx_pool = ctx.enter_context(tc.tile_pool(name="unit_mx", bufs=3))
+        feat_pool = ctx.enter_context(tc.tile_pool(name="feat", bufs=2))
+        feat_mx_pool = ctx.enter_context(tc.tile_pool(name="feat_mx", bufs=6))
+        prob_pool = ctx.enter_context(tc.tile_pool(name="prob", bufs=5))
+        small = ctx.enter_context(tc.tile_pool(name="small", bufs=5))
+        psum = ctx.enter_context(tc.psum_pool(name="psum", bufs=PSUM_BANKS))
+        ctx.enter_context(tc.manual_schedule())
+
+        def load_rows(chunk_views):
+            rows = rows_pool.tile([P, CHUNKS * WIDTH], BF16, name="rows")
+            for c in range(CHUNKS):
+                nc.sync.dma_start(out=rows[:, c * WIDTH : (c + 1) * WIDTH], in_=chunk_views[c])
+            return rows
+
+        def load_unit(unit):
+            source = q_lin if unit % 2 == 0 else k_lin
+            return load_rows([source[unit // 2, c * P : (c + 1) * P, :] for c in range(CHUNKS)])
+
+        def load_weight(weight):
+            by_chunk = weight.rearrange("(p c) d -> c p d", c=CHUNKS)
+            return load_rows([by_chunk[c] for c in range(CHUNKS)])
+
+        def transpose_rows(rows, call_no):
+            words = rows[:].bitcast(F32)
+            grouped = grouped_pool.tile(
+                [P, PASSES * TOKENS * PACK], BF16, name="grouped", align_bytes=64
+            )
+            grouped_words = grouped[:].bitcast(F32)
+            for g in range(PASSES):
+                for half in range(CHUNKS // 2):
+                    bank = psum.tile([P, BANK], F32, name="bank")
+                    for u in range(2):
+                        for j in range(2):
+                            first_word = (2 * half + j) * ROW_WORDS + g * PASS_WORDS + u
+                            nc.tensor.transpose(
+                                out=bank[:, (2 * u + j) * P : (2 * u + j + 1) * P],
+                                in_=words[:, first_word : first_word - u + PASS_WORDS : 2],
+                                identity=ident[:],
+                            )
+                    n = g * (CHUNKS // 2) + half
+                    target = grouped_words[:, n * BANK : (n + 1) * BANK].rearrange(
+                        "p (r u) -> p r u", u=2
+                    )
+                    planes = bank[:].rearrange("p (u r) -> p r u", u=2)
+                    if (call_no * UNIT_BANKS + n) % VECTOR_EVERY == VECTOR_EVERY - 1:
+                        nc.vector.tensor_copy(out=target, in_=planes)
+                    else:
+                        nc.scalar.copy(out=target, in_=planes)
+            return grouped
+
+        def quantise_rows(grouped, codes, scales):
+            nc.vector.quantize_mx(out=codes[:].bitcast(FP8X4), scales=scales[:], in_=grouped[:])
+
+        def new_unit_mx():
+            codes = unit_mx_pool.tile([P, PASSES * TOKENS], U32, name="unit_codes", align_bytes=64)
+            scales = unit_mx_pool.tile([P, PASSES * TOKENS], U8, name="unit_scales", align_bytes=64)
+            return codes, scales
+
+        def project(unit_mx, weight_mx):
+            codes, scales = unit_mx
+            w_codes, w_scales = weight_mx
+            feat = feat_pool.tile([P, TOKENS * PACK], BF16, name="feat", align_bytes=64)
+            for c in range(CHUNKS):
+                bank = psum.tile([P, BANK], F32, name="bank")
+                for t in range(PACK):
+                    for g in range(PASSES):
+                        w_cols = slice(g * FEATURES + t * P, g * FEATURES + (t + 1) * P)
+                        x_cols = slice(g * TOKENS + c * P, g * TOKENS + (c + 1) * P)
+                        nc.tensor.matmul_mx(
+                            out=bank[:, t * P : (t + 1) * P],
+                            lhsT=w_codes[:, w_cols].bitcast(FP8X4),
+                            lhsT_scale=w_scales[:, w_cols],
+                            rhs=codes[:, x_cols].bitcast(FP8X4),
+                            rhs_scale=scales[:, x_cols],
+                            start=(g == 0),
+                            stop=(g == PASSES - 1),
+                        )
+                nc.scalar.copy(
+                    out=feat[:, c * BANK : (c + 1) * BANK].rearrange("p (r t) -> p r t", t=PACK),
+                    in_=bank[:].rearrange("p (t r) -> p r t", t=PACK),
+                )
+            return feat
+
+        def quantise_features(feat):
+            codes = feat_mx_pool.tile([P, TOKENS], U32, name="feat_codes", align_bytes=64)
+            scales = feat_mx_pool.tile([P, TOKENS], U8, name="feat_scales", align_bytes=64)
+            nc.vector.quantize_mx(out=codes[:].bitcast(FP8X4), scales=scales[:], in_=feat[:])
+            return codes, scales
+
+        def build_caps():
+            for c in range(CHUNKS):
+                nc.vector.tensor_scalar(
+                    out=caps[:, c * TOKENS : (c + 1) * TOKENS],
+                    in0=mask_rows[:, 2 * c * TOKENS : 2 * (c + 1) * TOKENS : 2],
+                    scalar1=-2.0 * CAP,
+                    scalar2=CAP,
+                    op0=ALU.mult,
+                    op1=ALU.add,
+                )
+
+        def score_pair(pair, q_mx, k_mx):
+            q_codes, q_scales = q_mx
+            k_codes, k_scales = k_mx
+            prob = prob_pool.tile([P, PAIR * TOKENS], F32, name="prob")
+            negmax = small.tile([P, PAIR], F32, name="negmax")
+            for i in range(PAIR):
+                tile_no = (pair % (CHUNKS // PAIR)) * PAIR + i
+                bank = psum.tile([P, BANK], F32, name="bank")
+                nc.tensor.matmul_mx(
+                    out=bank[:],
+                    lhsT=q_codes[:, tile_no * P : (tile_no + 1) * P].bitcast(FP8X4),
+                    lhsT_scale=q_scales[:, tile_no * P : (tile_no + 1) * P],
+                    rhs=k_codes[:].bitcast(FP8X4),
+                    rhs_scale=k_scales[:],
+                    start=True,
+                    stop=True,
+                )
+                nc.vector.scalar_tensor_tensor(
+                    out=prob[:, i * TOKENS : (i + 1) * TOKENS],
+                    in0=bank[:],
+                    scalar=SCORE_SCALE,
+                    in1=caps[:, tile_no * TOKENS : (tile_no + 1) * TOKENS],
+                    op0=ALU.mult,
+                    op1=ALU.min,
+                )
+            for i in range(PAIR):
+                nc.vector.tensor_reduce(
+                    out=negmax[:, i : i + 1],
+                    in_=prob[:, i * TOKENS : (i + 1) * TOKENS],
+                    axis=mybir.AxisListType.X,
+                    op=ALU.max,
+                    negate=True,
+                )
+            return prob, negmax
+
+        def exponentials(prob, negmax):
+            rowsum = small.tile([P, PAIR], F32, name="rowsum")
+            for i in range(PAIR):
+                nc.scalar.activation(
+                    out=prob[:, i * TOKENS : (i + 1) * TOKENS],
+                    in_=prob[:, i * TOKENS : (i + 1) * TOKENS],
+                    func=ACT.Exp,
+                    bias=negmax[:, i : i + 1],
+                    scale=1.0,
+                    accum_out=rowsum[:, i : i + 1],
+                )
+            return rowsum
+
+        def normalise_and_store(pair, prob, rowsum):
+            inverse = small.tile([P, PAIR], F32, name="inverse")
+            nc.vector.reciprocal(out=inverse[:], in_=rowsum[:])
+            for i in range(PAIR):
+                tile_no = (pair % (CHUNKS // PAIR)) * PAIR + i
+                nc.gpsimd.tensor_scalar(
+                    out=prob[:, i * TOKENS : (i + 1) * TOKENS],
+                    in0=prob[:, i * TOKENS : (i + 1) * TOKENS],
+                    scalar1=inverse[:, i : i + 1],
+                    scalar2=0.0,
+                    op0=ALU.mult,
+                    op1=ALU.add,
+                )
+                nc.sync.dma_start(
+                    out=out[pair // (CHUNKS // PAIR), tile_no * P : (tile_no + 1) * P, :],
+                    in_=prob[:, i * TOKENS : (i + 1) * TOKENS],
+                )
+
+        ident = const.tile([P, P], F32, name="ident")
+        make_identity(nc, ident[:])
+        warm = const.tile([P, 1], F32, name="warm")
+        nc.vector.memset(warm[:], 0.0)
+        nc.scalar.activation(out=warm[:], in_=warm[:], func=ACT.Exp)
+
+        rows = {}
+        rotation_rows = load_weight(rotation_params)
+        rows[0] = load_unit(0)
+        entangle_rows = load_weight(entangle_params)
+        for unit in range(1, PREFETCH):
+            rows[unit] = load_unit(unit)
+        mask_rows = const.tile([P, CHUNKS * 2 * TOKENS], I32, name="mask_rows")
+        mask_words = mask.bitcast(I32)
+        for c in range(CHUNKS):
+            nc.sync.dma_start(
+                out=mask_rows[:, 2 * c * TOKENS : 2 * (c + 1) * TOKENS],
+                in_=mask_words[c * P : (c + 1) * P, :],
+            )
+        caps = const.tile([P, CHUNKS * TOKENS], F32, name="caps")
+
+        weight_mx = []
+        unit_mx = {}
+        for name in ("rotation", "entangle"):
+            weight_mx.append(
+                (
+                    const.tile([P, PASSES * FEATURES], U32, name=name + "_codes", align_bytes=64),
+                    const.tile([P, PASSES * FEATURES], U8, name=name + "_scales", align_bytes=64),
+                )
+            )
+        quantise_rows(transpose_rows(rotation_rows, 0), weight_mx[0][0], weight_mx[0][1])
+        unit_mx[0] = new_unit_mx()
+        quantise_rows(transpose_rows(rows[0], 1), unit_mx[0][0], unit_mx[0][1])
+        quantise_rows(transpose_rows(entangle_rows, 2), weight_mx[1][0], weight_mx[1][1])
+
+        feat_mx = {}
+        scored = {}
+        summed = {}
+        feat = {}
+        for step in range(UNITS + 4):
+            ahead = step + PREFETCH
+            following = step + 1
+            projected = step - 1
+            scoring = step - 2
+            raising = step - 3
+            dividing = step - 4
+            if ahead < UNITS:
+                rows[ahead] = load_unit(ahead)
+            if following < UNITS:
+                grouped = transpose_rows(rows[following], following + 2)
+            if 0 <= projected < UNITS:
+                feat_mx[projected] = quantise_features(feat[projected])
+            if following < UNITS:
+                unit_mx[following] = new_unit_mx()
+                quantise_rows(grouped, unit_mx[following][0], unit_mx[following][1])
+            if 0 <= dividing < PAIRS:
+                normalise_and_store(dividing, scored[dividing][0], summed[dividing])
+            if step < UNITS:
+                feat[step] = project(unit_mx[step], weight_mx[step % 2])
+            if 0 <= raising < PAIRS:
+                summed[raising] = exponentials(scored[raising][0], scored[raising][1])
+            if scoring == 0:
+                build_caps()
+            if 0 <= scoring < PAIRS:
+                b = scoring // (CHUNKS // PAIR)
+                scored[scoring] = score_pair(scoring, feat_mx[2 * b], feat_mx[2 * b + 1])

@@ -26,11 +26,12 @@ CHUNKS = TOKENS // P
 PASSES = WIDTH // K_PASS
 ROW_WORDS = WIDTH // 2
 PASS_WORDS = K_PASS // 2
+CHUNK_COLS = PASSES * P
 UNITS = 2 * BATCH
+LAST = UNITS - 1
 PAIR = 2
 PAIRS = BATCH * CHUNKS // PAIR
 PREFETCH = 4
-UNIT_BANKS = PASSES * CHUNKS // 2
 VECTOR_EVERY = 3
 
 SCORE_SCALE = 1.0 / 32.0
@@ -51,7 +52,8 @@ def tile_selfattention_pa_t_kernel(
         feat_pool = ctx.enter_context(tc.tile_pool(name="feat", bufs=2))
         feat_mx_pool = ctx.enter_context(tc.tile_pool(name="feat_mx", bufs=6))
         prob_pool = ctx.enter_context(tc.tile_pool(name="prob", bufs=5))
-        small = ctx.enter_context(tc.tile_pool(name="small", bufs=5))
+        last_prob_pool = ctx.enter_context(tc.tile_pool(name="last_prob", bufs=CHUNKS))
+        small = ctx.enter_context(tc.tile_pool(name="small", bufs=8))
         psum = ctx.enter_context(tc.psum_pool(name="psum", bufs=PSUM_BANKS))
         ctx.enter_context(tc.manual_schedule())
 
@@ -62,7 +64,7 @@ def tile_selfattention_pa_t_kernel(
             return rows
 
         def load_unit(unit):
-            source = q_lin if unit % 2 == 0 else k_lin
+            source = k_lin if unit % 2 == 0 else q_lin
             return load_rows([source[unit // 2, c * P : (c + 1) * P, :] for c in range(CHUNKS)])
 
         def load_weight(weight):
@@ -75,66 +77,78 @@ def tile_selfattention_pa_t_kernel(
                 [P, PASSES * TOKENS * PACK], BF16, name="grouped", align_bytes=64
             )
             grouped_words = grouped[:].bitcast(F32)
-            for g in range(PASSES):
-                for half in range(CHUNKS // 2):
-                    bank = psum.tile([P, BANK], F32, name="bank")
+            for c in range(CHUNKS):
+                bank = psum.tile([P, BANK], F32, name="bank")
+                for g in range(PASSES):
                     for u in range(2):
-                        for j in range(2):
-                            first_word = (2 * half + j) * ROW_WORDS + g * PASS_WORDS + u
-                            nc.tensor.transpose(
-                                out=bank[:, (2 * u + j) * P : (2 * u + j + 1) * P],
-                                in_=words[:, first_word : first_word - u + PASS_WORDS : 2],
-                                identity=ident[:],
-                            )
-                    n = g * (CHUNKS // 2) + half
-                    target = grouped_words[:, n * BANK : (n + 1) * BANK].rearrange(
-                        "p (r u) -> p r u", u=2
-                    )
-                    planes = bank[:].rearrange("p (u r) -> p r u", u=2)
-                    if (call_no * UNIT_BANKS + n) % VECTOR_EVERY == VECTOR_EVERY - 1:
-                        nc.vector.tensor_copy(out=target, in_=planes)
-                    else:
-                        nc.scalar.copy(out=target, in_=planes)
+                        first_word = c * ROW_WORDS + g * PASS_WORDS
+                        nc.tensor.transpose(
+                            out=bank[:, (2 * g + u) * P : (2 * g + u + 1) * P],
+                            in_=words[:, first_word + u : first_word + PASS_WORDS : 2],
+                            identity=ident[:],
+                        )
+                target = grouped_words[:, c * BANK : (c + 1) * BANK].rearrange(
+                    "p (g r u) -> p g r u", g=PASSES, u=2
+                )
+                halves = bank[:].rearrange("p (g u r) -> p g r u", g=PASSES, u=2)
+                if (call_no * CHUNKS + c) % VECTOR_EVERY == VECTOR_EVERY - 1:
+                    nc.vector.tensor_copy(out=target, in_=halves)
+                else:
+                    nc.scalar.copy(out=target, in_=halves)
             return grouped
 
-        def quantise_rows(grouped, codes, scales):
-            nc.vector.quantize_mx(out=codes[:].bitcast(FP8X4), scales=scales[:], in_=grouped[:])
+        def quantise_rows(grouped, row_mx, first_chunk=0, end_chunk=CHUNKS):
+            codes, scales = row_mx
+            cols = slice(first_chunk * CHUNK_COLS, end_chunk * CHUNK_COLS)
+            nc.vector.quantize_mx(
+                out=codes[:, cols].bitcast(FP8X4),
+                scales=scales[:, cols],
+                in_=grouped[:, cols.start * PACK : cols.stop * PACK],
+            )
 
         def new_unit_mx():
             codes = unit_mx_pool.tile([P, PASSES * TOKENS], U32, name="unit_codes", align_bytes=64)
             scales = unit_mx_pool.tile([P, PASSES * TOKENS], U8, name="unit_scales", align_bytes=64)
             return codes, scales
 
-        def project(unit_mx, weight_mx):
-            codes, scales = unit_mx
-            w_codes, w_scales = weight_mx
-            feat = feat_pool.tile([P, TOKENS * PACK], BF16, name="feat", align_bytes=64)
-            for c in range(CHUNKS):
-                bank = psum.tile([P, BANK], F32, name="bank")
-                for t in range(PACK):
-                    for g in range(PASSES):
-                        w_cols = slice(g * FEATURES + t * P, g * FEATURES + (t + 1) * P)
-                        x_cols = slice(g * TOKENS + c * P, g * TOKENS + (c + 1) * P)
-                        nc.tensor.matmul_mx(
-                            out=bank[:, t * P : (t + 1) * P],
-                            lhsT=w_codes[:, w_cols].bitcast(FP8X4),
-                            lhsT_scale=w_scales[:, w_cols],
-                            rhs=codes[:, x_cols].bitcast(FP8X4),
-                            rhs_scale=scales[:, x_cols],
-                            start=(g == 0),
-                            stop=(g == PASSES - 1),
-                        )
-                nc.scalar.copy(
-                    out=feat[:, c * BANK : (c + 1) * BANK].rearrange("p (r t) -> p r t", t=PACK),
-                    in_=bank[:].rearrange("p (t r) -> p r t", t=PACK),
-                )
-            return feat
+        def new_feat():
+            return feat_pool.tile([P, TOKENS * PACK], BF16, name="feat", align_bytes=64)
 
-        def quantise_features(feat):
+        def new_feat_mx():
             codes = feat_mx_pool.tile([P, TOKENS], U32, name="feat_codes", align_bytes=64)
             scales = feat_mx_pool.tile([P, TOKENS], U8, name="feat_scales", align_bytes=64)
-            nc.vector.quantize_mx(out=codes[:].bitcast(FP8X4), scales=scales[:], in_=feat[:])
             return codes, scales
+
+        def project_chunk(c, unit_mx, weight_mx, feat):
+            codes, scales = unit_mx
+            w_codes, w_scales = weight_mx
+            bank = psum.tile([P, BANK], F32, name="bank")
+            for t in range(PACK):
+                for g in range(PASSES):
+                    w_cols = slice(t * CHUNK_COLS + g * P, t * CHUNK_COLS + (g + 1) * P)
+                    x_cols = slice(c * CHUNK_COLS + g * P, c * CHUNK_COLS + (g + 1) * P)
+                    nc.tensor.matmul_mx(
+                        out=bank[:, t * P : (t + 1) * P],
+                        lhsT=w_codes[:, w_cols].bitcast(FP8X4),
+                        lhsT_scale=w_scales[:, w_cols],
+                        rhs=codes[:, x_cols].bitcast(FP8X4),
+                        rhs_scale=scales[:, x_cols],
+                        start=(g == 0),
+                        stop=(g == PASSES - 1),
+                    )
+            nc.scalar.copy(
+                out=feat[:, c * BANK : (c + 1) * BANK].rearrange("p (r t) -> p r t", t=PACK),
+                in_=bank[:].rearrange("p (t r) -> p r t", t=PACK),
+            )
+
+        def quantise_features(feat, feat_mx, first_token=0, end_token=TOKENS):
+            codes, scales = feat_mx
+            cols = slice(first_token, end_token)
+            nc.vector.quantize_mx(
+                out=codes[:, cols].bitcast(FP8X4),
+                scales=scales[:, cols],
+                in_=feat[:, first_token * PACK : end_token * PACK],
+            )
 
         def build_caps():
             for c in range(CHUNKS):
@@ -147,71 +161,101 @@ def tile_selfattention_pa_t_kernel(
                     op1=ALU.add,
                 )
 
-        def score_pair(pair, q_mx, k_mx):
+        def new_softmax(pool=prob_pool, tiles=PAIR):
+            prob = pool.tile([P, tiles * TOKENS], F32, name="prob")
+            negmax = small.tile([P, tiles], F32, name="negmax")
+            rowsum = small.tile([P, tiles], F32, name="rowsum")
+            inverse = small.tile([P, tiles], F32, name="inverse")
+            return prob, negmax, rowsum, inverse
+
+        def score_tile(tile_no, q_mx, k_mx):
             q_codes, q_scales = q_mx
             k_codes, k_scales = k_mx
-            prob = prob_pool.tile([P, PAIR * TOKENS], F32, name="prob")
-            negmax = small.tile([P, PAIR], F32, name="negmax")
-            for i in range(PAIR):
-                tile_no = (pair % (CHUNKS // PAIR)) * PAIR + i
-                bank = psum.tile([P, BANK], F32, name="bank")
-                nc.tensor.matmul_mx(
-                    out=bank[:],
-                    lhsT=q_codes[:, tile_no * P : (tile_no + 1) * P].bitcast(FP8X4),
-                    lhsT_scale=q_scales[:, tile_no * P : (tile_no + 1) * P],
-                    rhs=k_codes[:].bitcast(FP8X4),
-                    rhs_scale=k_scales[:],
-                    start=True,
-                    stop=True,
-                )
-                nc.vector.scalar_tensor_tensor(
-                    out=prob[:, i * TOKENS : (i + 1) * TOKENS],
-                    in0=bank[:],
-                    scalar=SCORE_SCALE,
-                    in1=caps[:, tile_no * TOKENS : (tile_no + 1) * TOKENS],
-                    op0=ALU.mult,
-                    op1=ALU.min,
-                )
-            for i in range(PAIR):
-                nc.vector.tensor_reduce(
-                    out=negmax[:, i : i + 1],
-                    in_=prob[:, i * TOKENS : (i + 1) * TOKENS],
-                    axis=mybir.AxisListType.X,
-                    op=ALU.max,
-                    negate=True,
-                )
-            return prob, negmax
+            bank = psum.tile([P, BANK], F32, name="bank")
+            nc.tensor.matmul_mx(
+                out=bank[:],
+                lhsT=q_codes[:, tile_no * P : (tile_no + 1) * P].bitcast(FP8X4),
+                lhsT_scale=q_scales[:, tile_no * P : (tile_no + 1) * P],
+                rhs=k_codes[:].bitcast(FP8X4),
+                rhs_scale=k_scales[:],
+                start=True,
+                stop=True,
+            )
+            return bank
 
-        def exponentials(prob, negmax):
-            rowsum = small.tile([P, PAIR], F32, name="rowsum")
-            for i in range(PAIR):
-                nc.scalar.activation(
-                    out=prob[:, i * TOKENS : (i + 1) * TOKENS],
-                    in_=prob[:, i * TOKENS : (i + 1) * TOKENS],
-                    func=ACT.Exp,
-                    bias=negmax[:, i : i + 1],
-                    scale=1.0,
-                    accum_out=rowsum[:, i : i + 1],
-                )
-            return rowsum
+        def mask_scores(bank, tile_no, i, softmax):
+            nc.vector.scalar_tensor_tensor(
+                out=softmax[0][:, i * TOKENS : (i + 1) * TOKENS],
+                in0=bank[:],
+                scalar=SCORE_SCALE,
+                in1=caps[:, tile_no * TOKENS : (tile_no + 1) * TOKENS],
+                op0=ALU.mult,
+                op1=ALU.min,
+            )
 
-        def normalise_and_store(pair, prob, rowsum):
-            inverse = small.tile([P, PAIR], F32, name="inverse")
-            nc.vector.reciprocal(out=inverse[:], in_=rowsum[:])
+        def row_maximum(i, softmax):
+            prob, negmax = softmax[0], softmax[1]
+            nc.vector.tensor_reduce(
+                out=negmax[:, i : i + 1],
+                in_=prob[:, i * TOKENS : (i + 1) * TOKENS],
+                axis=mybir.AxisListType.X,
+                op=ALU.max,
+                negate=True,
+            )
+
+        def exponential(i, softmax):
+            prob, negmax, rowsum = softmax[0], softmax[1], softmax[2]
+            nc.scalar.activation(
+                out=prob[:, i * TOKENS : (i + 1) * TOKENS],
+                in_=prob[:, i * TOKENS : (i + 1) * TOKENS],
+                func=ACT.Exp,
+                bias=negmax[:, i : i + 1],
+                scale=1.0,
+                accum_out=rowsum[:, i : i + 1],
+            )
+
+        def invert(softmax):
+            nc.vector.reciprocal(out=softmax[3][:], in_=softmax[2][:])
+
+        def divide(i, softmax, engine):
+            prob, inverse = softmax[0], softmax[3]
+            engine.tensor_scalar(
+                out=prob[:, i * TOKENS : (i + 1) * TOKENS],
+                in0=prob[:, i * TOKENS : (i + 1) * TOKENS],
+                scalar1=inverse[:, i : i + 1],
+                scalar2=0.0,
+                op0=ALU.mult,
+                op1=ALU.add,
+            )
+
+        def store(b, tile_no, i, softmax):
+            nc.sync.dma_start(
+                out=out[b, tile_no * P : (tile_no + 1) * P, :],
+                in_=softmax[0][:, i * TOKENS : (i + 1) * TOKENS],
+            )
+
+        def score_pair(pair):
+            b, first = divmod(pair * PAIR, CHUNKS)
+            softmax = new_softmax()
             for i in range(PAIR):
-                tile_no = (pair % (CHUNKS // PAIR)) * PAIR + i
-                nc.gpsimd.tensor_scalar(
-                    out=prob[:, i * TOKENS : (i + 1) * TOKENS],
-                    in0=prob[:, i * TOKENS : (i + 1) * TOKENS],
-                    scalar1=inverse[:, i : i + 1],
-                    scalar2=0.0,
-                    op0=ALU.mult,
-                    op1=ALU.add,
-                )
-                nc.sync.dma_start(
-                    out=out[pair // (CHUNKS // PAIR), tile_no * P : (tile_no + 1) * P, :],
-                    in_=prob[:, i * TOKENS : (i + 1) * TOKENS],
-                )
+                bank = score_tile(first + i, feat_mx[2 * b + 1], feat_mx[2 * b])
+                mask_scores(bank, first + i, i, softmax)
+            return softmax
+
+        def find_maxima(softmax):
+            for i in range(PAIR):
+                row_maximum(i, softmax)
+
+        def exponentials(softmax):
+            for i in range(PAIR):
+                exponential(i, softmax)
+
+        def normalise_and_store(pair, softmax):
+            b, first = divmod(pair * PAIR, CHUNKS)
+            invert(softmax)
+            for i in range(PAIR):
+                divide(i, softmax, nc.gpsimd)
+                store(b, first + i, i, softmax)
 
         ident = const.tile([P, P], F32, name="ident")
         make_identity(nc, ident[:])
@@ -220,9 +264,9 @@ def tile_selfattention_pa_t_kernel(
         nc.scalar.activation(out=warm[:], in_=warm[:], func=ACT.Exp)
 
         rows = {}
-        rotation_rows = load_weight(rotation_params)
-        rows[0] = load_unit(0)
         entangle_rows = load_weight(entangle_params)
+        rows[0] = load_unit(0)
+        rotation_rows = load_weight(rotation_params)
         for unit in range(1, PREFETCH):
             rows[unit] = load_unit(unit)
         mask_rows = const.tile([P, CHUNKS * 2 * TOKENS], I32, name="mask_rows")
@@ -236,26 +280,23 @@ def tile_selfattention_pa_t_kernel(
 
         weight_mx = []
         unit_mx = {}
-        for name in ("rotation", "entangle"):
+        for name in ("entangle", "rotation"):
             weight_mx.append(
                 (
                     const.tile([P, PASSES * FEATURES], U32, name=name + "_codes", align_bytes=64),
                     const.tile([P, PASSES * FEATURES], U8, name=name + "_scales", align_bytes=64),
                 )
             )
-        quantise_rows(transpose_rows(rotation_rows, 0), weight_mx[0][0], weight_mx[0][1])
+        quantise_rows(transpose_rows(entangle_rows, 0), weight_mx[0])
         unit_mx[0] = new_unit_mx()
-        quantise_rows(transpose_rows(rows[0], 1), unit_mx[0][0], unit_mx[0][1])
-        quantise_rows(transpose_rows(entangle_rows, 2), weight_mx[1][0], weight_mx[1][1])
+        quantise_rows(transpose_rows(rows[0], 1), unit_mx[0])
+        quantise_rows(transpose_rows(rotation_rows, 2), weight_mx[1])
 
         feat_mx = {}
-        scored = {}
-        summed = {}
-        feat = {}
-        for step in range(UNITS + 4):
+        softmax = {}
+        for step in range(UNITS):
             ahead = step + PREFETCH
             following = step + 1
-            projected = step - 1
             scoring = step - 2
             raising = step - 3
             dividing = step - 4
@@ -263,19 +304,51 @@ def tile_selfattention_pa_t_kernel(
                 rows[ahead] = load_unit(ahead)
             if following < UNITS:
                 grouped = transpose_rows(rows[following], following + 2)
-            if 0 <= projected < UNITS:
-                feat_mx[projected] = quantise_features(feat[projected])
-            if following < UNITS:
-                unit_mx[following] = new_unit_mx()
-                quantise_rows(grouped, unit_mx[following][0], unit_mx[following][1])
-            if 0 <= dividing < PAIRS:
-                normalise_and_store(dividing, scored[dividing][0], summed[dividing])
-            if step < UNITS:
-                feat[step] = project(unit_mx[step], weight_mx[step % 2])
-            if 0 <= raising < PAIRS:
-                summed[raising] = exponentials(scored[raising][0], scored[raising][1])
             if scoring == 0:
                 build_caps()
-            if 0 <= scoring < PAIRS:
-                b = scoring // (CHUNKS // PAIR)
-                scored[scoring] = score_pair(scoring, feat_mx[2 * b], feat_mx[2 * b + 1])
+            if 0 <= scoring < PAIRS - 3:
+                softmax[scoring] = score_pair(scoring)
+            if following < UNITS:
+                unit_mx[following] = new_unit_mx()
+                quantise_rows(grouped, unit_mx[following])
+            if 0 <= dividing < PAIRS - 5:
+                normalise_and_store(dividing, softmax[dividing])
+            feat = new_feat()
+            for c in range(CHUNKS):
+                project_chunk(c, unit_mx[step], weight_mx[step % 2], feat)
+            if 0 <= scoring < PAIRS - 3:
+                find_maxima(softmax[scoring])
+            if raising >= 0:
+                exponentials(softmax[raising])
+            if step == LAST - 1:
+                softmax[scoring + 1] = score_pair(scoring + 1)
+            feat_mx[step] = new_feat_mx()
+            if step < LAST:
+                quantise_features(feat, feat_mx[step])
+            if step == LAST - 1:
+                find_maxima(softmax[scoring + 1])
+
+        per_half = CHUNKS // 2
+        before = softmax[PAIRS - 3]
+        tiles = [new_softmax(last_prob_pool, 1) for c in range(CHUNKS)]
+        quantise_features(feat, feat_mx[LAST], 0, per_half * P)
+        quantise_features(feat, feat_mx[LAST], per_half * P, TOKENS)
+        banks = [score_tile(c, feat_mx[LAST], feat_mx[LAST - 1]) for c in range(CHUNKS)]
+        exponentials(before)
+        normalise_and_store(PAIRS - 5, softmax[PAIRS - 5])
+        mask_scores(banks[0], 0, 0, tiles[0])
+        normalise_and_store(PAIRS - 4, softmax[PAIRS - 4])
+        for c in range(CHUNKS):
+            if c + 1 < CHUNKS:
+                mask_scores(banks[c + 1], c + 1, 0, tiles[c + 1])
+            row_maximum(0, tiles[c])
+            exponential(0, tiles[c])
+            if c == 0:
+                normalise_and_store(PAIRS - 3, before)
+            else:
+                invert(tiles[c - 1])
+                divide(0, tiles[c - 1], nc.gpsimd)
+                store(BATCH - 1, c - 1, 0, tiles[c - 1])
+        invert(tiles[CHUNKS - 1])
+        divide(0, tiles[CHUNKS - 1], nc.vector)
+        store(BATCH - 1, CHUNKS - 1, 0, tiles[CHUNKS - 1])

@@ -32,7 +32,8 @@ LAST = UNITS - 1
 PAIR = 2
 PAIRS = BATCH * CHUNKS // PAIR
 PREFETCH = 4
-VECTOR_EVERY = 3
+VECTOR_FROM = 5
+VECTOR_CHUNK = 1
 
 SCORE_SCALE = 1.0 / 32.0
 CAP = 1.0e38
@@ -71,7 +72,7 @@ def tile_selfattention_pa_t_kernel(
             by_chunk = weight.rearrange("(p c) d -> c p d", c=CHUNKS)
             return load_rows([by_chunk[c] for c in range(CHUNKS)])
 
-        def transpose_rows(rows, call_no):
+        def transpose_rows(rows, unit=-1):
             words = rows[:].bitcast(F32)
             grouped = grouped_pool.tile(
                 [P, PASSES * TOKENS * PACK], BF16, name="grouped", align_bytes=64
@@ -91,7 +92,7 @@ def tile_selfattention_pa_t_kernel(
                     "p (g r u) -> p g r u", g=PASSES, u=2
                 )
                 halves = bank[:].rearrange("p (g u r) -> p g r u", g=PASSES, u=2)
-                if (call_no * CHUNKS + c) % VECTOR_EVERY == VECTOR_EVERY - 1:
+                if unit >= VECTOR_FROM and c == VECTOR_CHUNK:
                     nc.vector.tensor_copy(out=target, in_=halves)
                 else:
                     nc.scalar.copy(out=target, in_=halves)
@@ -243,8 +244,13 @@ def tile_selfattention_pa_t_kernel(
             return softmax
 
         def find_maxima(softmax):
-            for i in range(PAIR):
-                row_maximum(i, softmax)
+            nc.vector.tensor_reduce(
+                out=softmax[1][:],
+                in_=softmax[0][:].rearrange("p (i k) -> p i k", i=PAIR),
+                axis=mybir.AxisListType.X,
+                op=ALU.max,
+                negate=True,
+            )
 
         def exponentials(softmax):
             for i in range(PAIR):
@@ -287,10 +293,10 @@ def tile_selfattention_pa_t_kernel(
                     const.tile([P, PASSES * FEATURES], U8, name=name + "_scales", align_bytes=64),
                 )
             )
-        quantise_rows(transpose_rows(entangle_rows, 0), weight_mx[0])
+        quantise_rows(transpose_rows(entangle_rows), weight_mx[0])
         unit_mx[0] = new_unit_mx()
-        quantise_rows(transpose_rows(rows[0], 1), unit_mx[0])
-        quantise_rows(transpose_rows(rotation_rows, 2), weight_mx[1])
+        quantise_rows(transpose_rows(rows[0], 0), unit_mx[0])
+        quantise_rows(transpose_rows(rotation_rows), weight_mx[1])
 
         feat_mx = {}
         softmax = {}
@@ -303,7 +309,7 @@ def tile_selfattention_pa_t_kernel(
             if ahead < UNITS:
                 rows[ahead] = load_unit(ahead)
             if following < UNITS:
-                grouped = transpose_rows(rows[following], following + 2)
+                grouped = transpose_rows(rows[following], following)
             if scoring == 0:
                 build_caps()
             if 0 <= scoring < PAIRS - 3:

@@ -32,6 +32,7 @@ LAST = UNITS - 1
 PAIR = 2
 PAIRS = BATCH * CHUNKS // PAIR
 PREFETCH = 4
+ORDERED_CHUNK = 3
 VECTOR_FROM = 5
 VECTOR_CHUNK = 1
 
@@ -48,6 +49,7 @@ def tile_selfattention_pa_t_kernel(
     with ExitStack() as ctx:
         const = ctx.enter_context(tc.tile_pool(name="const", bufs=1))
         rows_pool = ctx.enter_context(tc.tile_pool(name="rows", bufs=PREFETCH + 2))
+        ordered_pool = ctx.enter_context(tc.tile_pool(name="ordered", bufs=3))
         grouped_pool = ctx.enter_context(tc.tile_pool(name="grouped", bufs=2))
         unit_mx_pool = ctx.enter_context(tc.tile_pool(name="unit_mx", bufs=3))
         feat_pool = ctx.enter_context(tc.tile_pool(name="feat", bufs=2))
@@ -72,7 +74,22 @@ def tile_selfattention_pa_t_kernel(
             by_chunk = weight.rearrange("(p c) d -> c p d", c=CHUNKS)
             return load_rows([by_chunk[c] for c in range(CHUNKS)])
 
-        def transpose_rows(rows, unit=-1):
+        def order_words(rows):
+            ordered = ordered_pool.tile([P, WIDTH], BF16, name="ordered")
+            one = small.tile([P, 1], F32, name="one")
+            nc.vector.memset(one[:], 1.0)
+            chunk = rows[:, ORDERED_CHUNK * WIDTH : (ORDERED_CHUNK + 1) * WIDTH]
+            nc.gpsimd.tensor_scalar(
+                out=ordered[:].rearrange("p (u m e) -> p u m e", u=2, e=2),
+                in0=chunk.rearrange("p (m u e) -> p u m e", u=2, e=2),
+                scalar1=one[:],
+                scalar2=0.0,
+                op0=ALU.mult,
+                op1=ALU.add,
+            )
+            return ordered
+
+        def transpose_rows(rows, unit=-1, ordered=None):
             words = rows[:].bitcast(F32)
             grouped = grouped_pool.tile(
                 [P, PASSES * TOKENS * PACK], BF16, name="grouped", align_bytes=64
@@ -82,10 +99,15 @@ def tile_selfattention_pa_t_kernel(
                 bank = psum.tile([P, BANK], F32, name="bank")
                 for g in range(PASSES):
                     for u in range(2):
-                        first_word = c * ROW_WORDS + g * PASS_WORDS
+                        if ordered is not None and c == ORDERED_CHUNK:
+                            first_word = (u * PASSES + g) * P
+                            every_second = ordered[:].bitcast(F32)[:, first_word : first_word + P]
+                        else:
+                            first_word = c * ROW_WORDS + g * PASS_WORDS
+                            every_second = words[:, first_word + u : first_word + PASS_WORDS : 2]
                         nc.tensor.transpose(
                             out=bank[:, (2 * g + u) * P : (2 * g + u + 1) * P],
-                            in_=words[:, first_word + u : first_word + PASS_WORDS : 2],
+                            in_=every_second,
                             identity=ident[:],
                         )
                 target = grouped_words[:, c * BANK : (c + 1) * BANK].rearrange(
@@ -300,6 +322,7 @@ def tile_selfattention_pa_t_kernel(
 
         feat_mx = {}
         softmax = {}
+        ordered = ordered_next = None
         for step in range(UNITS):
             ahead = step + PREFETCH
             following = step + 1
@@ -309,7 +332,7 @@ def tile_selfattention_pa_t_kernel(
             if ahead < UNITS:
                 rows[ahead] = load_unit(ahead)
             if following < UNITS:
-                grouped = transpose_rows(rows[following], following)
+                grouped = transpose_rows(rows[following], following, ordered)
             if scoring == 0:
                 build_caps()
             if 0 <= scoring < PAIRS - 3:
@@ -331,6 +354,8 @@ def tile_selfattention_pa_t_kernel(
             feat_mx[step] = new_feat_mx()
             if step < LAST:
                 quantise_features(feat, feat_mx[step])
+            ordered = ordered_next
+            ordered_next = order_words(rows[following + 2]) if 2 <= following + 2 < UNITS else None
             if step == LAST - 1:
                 find_maxima(softmax[scoring + 1])
 

@@ -61,7 +61,7 @@ def tile_selfattention_pa_t_kernel(
         ctx.enter_context(tc.manual_schedule())
 
         def load_rows(chunk_views):
-            rows = rows_pool.tile([P, CHUNKS * WIDTH], BF16, name="rows")
+            rows = rows_pool.tile([P, CHUNKS * WIDTH], BF16, name="rows", align_bytes=256)
             for c in range(CHUNKS):
                 nc.sync.dma_start(out=rows[:, c * WIDTH : (c + 1) * WIDTH], in_=chunk_views[c])
             return rows
@@ -75,7 +75,7 @@ def tile_selfattention_pa_t_kernel(
             return load_rows([by_chunk[c] for c in range(CHUNKS)])
 
         def order_words(rows):
-            ordered = ordered_pool.tile([P, WIDTH], BF16, name="ordered")
+            ordered = ordered_pool.tile([P, WIDTH], BF16, name="ordered", align_bytes=256)
             one = small.tile([P, 1], F32, name="one")
             nc.vector.memset(one[:], 1.0)
             chunk = rows[:, ORDERED_CHUNK * WIDTH : (ORDERED_CHUNK + 1) * WIDTH]
@@ -92,7 +92,7 @@ def tile_selfattention_pa_t_kernel(
         def transpose_rows(rows, unit=-1, ordered=None):
             words = rows[:].bitcast(F32)
             grouped = grouped_pool.tile(
-                [P, PASSES * TOKENS * PACK], BF16, name="grouped", align_bytes=64
+                [P, PASSES * TOKENS * PACK], BF16, name="grouped", align_bytes=256
             )
             grouped_words = grouped[:].bitcast(F32)
             for c in range(CHUNKS):
@@ -130,16 +130,16 @@ def tile_selfattention_pa_t_kernel(
             )
 
         def new_unit_mx():
-            codes = unit_mx_pool.tile([P, PASSES * TOKENS], U32, name="unit_codes", align_bytes=64)
-            scales = unit_mx_pool.tile([P, PASSES * TOKENS], U8, name="unit_scales", align_bytes=64)
+            codes = unit_mx_pool.tile([P, PASSES * TOKENS], U32, name="unit_codes", align_bytes=256)
+            scales = unit_mx_pool.tile([P, PASSES * TOKENS], U8, name="unit_scales", align_bytes=256)
             return codes, scales
 
         def new_feat():
-            return feat_pool.tile([P, TOKENS * PACK], BF16, name="feat", align_bytes=64)
+            return feat_pool.tile([P, TOKENS * PACK], BF16, name="feat", align_bytes=256)
 
         def new_feat_mx():
-            codes = feat_mx_pool.tile([P, TOKENS], U32, name="feat_codes", align_bytes=64)
-            scales = feat_mx_pool.tile([P, TOKENS], U8, name="feat_scales", align_bytes=64)
+            codes = feat_mx_pool.tile([P, TOKENS], U32, name="feat_codes", align_bytes=256)
+            scales = feat_mx_pool.tile([P, TOKENS], U8, name="feat_scales", align_bytes=256)
             return codes, scales
 
         def project_chunk(c, unit_mx, weight_mx, feat):
@@ -285,7 +285,7 @@ def tile_selfattention_pa_t_kernel(
                 divide(i, softmax, nc.gpsimd)
                 store(b, first + i, i, softmax)
 
-        ident = const.tile([P, P], F32, name="ident")
+        ident = const.tile([P, P], F32, name="ident", align_bytes=256)
         make_identity(nc, ident[:])
         warm = const.tile([P, 1], F32, name="warm")
         nc.vector.memset(warm[:], 0.0)
@@ -311,8 +311,8 @@ def tile_selfattention_pa_t_kernel(
         for name in ("entangle", "rotation"):
             weight_mx.append(
                 (
-                    const.tile([P, PASSES * FEATURES], U32, name=name + "_codes", align_bytes=64),
-                    const.tile([P, PASSES * FEATURES], U8, name=name + "_scales", align_bytes=64),
+                    const.tile([P, PASSES * FEATURES], U32, name=name + "_codes", align_bytes=256),
+                    const.tile([P, PASSES * FEATURES], U8, name=name + "_scales", align_bytes=256),
                 )
             )
         quantise_rows(transpose_rows(entangle_rows), weight_mx[0])

from contextlib import ExitStack

import concourse.mybir as mybir
from concourse.masks import make_identity

F32 = mybir.dt.float32
BF16 = mybir.dt.bfloat16
I32 = mybir.dt.int32
U32 = mybir.dt.uint32
U8 = mybir.dt.uint8
FP8X4 = mybir.dt.float8_e4m3fn_x4
ALU = mybir.AluOpType
ACT = mybir.ActivationFunctionType

P = 128
PACK = 4
K_PASS = P * PACK
BANK = 512
PSUM_BANKS = 8

BATCH = 8
TOKENS = 512
WIDTH = 1024
FEATURES = 512
CHUNKS = TOKENS // P
PASSES = WIDTH // K_PASS
ROW_WORDS = WIDTH // 2
PASS_WORDS = K_PASS // 2
CHUNK_COLS = PASSES * P
UNITS = 2 * BATCH
LAST = UNITS - 1
PAIR = 2
PAIRS = BATCH * CHUNKS // PAIR
PREFETCH = 4
ORDERED_CHUNK = 3
VECTOR_FROM = 5
VECTOR_CHUNK = 1

SCORE_SCALE = 1.0 / 32.0
CAP = 1.0e38

FLOPS = 2 * (2 * BATCH * TOKENS * WIDTH * FEATURES) + 2 * BATCH * TOKENS * TOKENS * FEATURES


def tile_selfattention_pa_t_kernel(
    tc, q_lin, k_lin, rotation_params, entangle_params, mask, out
):
    nc = tc.nc
    with ExitStack() as ctx:
        const = ctx.enter_context(tc.tile_pool(name="const", bufs=1))
        rows_pool = ctx.enter_context(tc.tile_pool(name="rows", bufs=PREFETCH + 2))
        ordered_pool = ctx.enter_context(tc.tile_pool(name="ordered", bufs=3))
        grouped_pool = ctx.enter_context(tc.tile_pool(name="grouped", bufs=2))
        unit_mx_pool = ctx.enter_context(tc.tile_pool(name="unit_mx", bufs=3))
        feat_pool = ctx.enter_context(tc.tile_pool(name="feat", bufs=2))
        feat_mx_pool = ctx.enter_context(tc.tile_pool(name="feat_mx", bufs=6))
        prob_pool = ctx.enter_context(tc.tile_pool(name="prob", bufs=5))
        last_prob_pool = ctx.enter_context(tc.tile_pool(name="last_prob", bufs=CHUNKS))
        small = ctx.enter_context(tc.tile_pool(name="small", bufs=8))
        psum = ctx.enter_context(tc.psum_pool(name="psum", bufs=PSUM_BANKS))
        ctx.enter_context(tc.manual_schedule())

        def load_rows(chunk_views):
            rows = rows_pool.tile([P, CHUNKS * WIDTH], BF16, name="rows", align_bytes=256)
            for c in range(CHUNKS):
                nc.sync.dma_start(out=rows[:, c * WIDTH : (c + 1) * WIDTH], in_=chunk_views[c])
            return rows

        def load_unit(unit):
            source = k_lin if unit % 2 == 0 else q_lin
            return load_rows([source[unit // 2, c * P : (c + 1) * P, :] for c in range(CHUNKS)])

        def load_weight(weight):
            by_chunk = weight.rearrange("(p c) d -> c p d", c=CHUNKS)
            return load_rows([by_chunk[c] for c in range(CHUNKS)])

        def order_words(rows):
            ordered = ordered_pool.tile([P, WIDTH], BF16, name="ordered", align_bytes=256)
            one = small.tile([P, 1], F32, name="one")
            nc.vector.memset(one[:], 1.0)
            chunk = rows[:, ORDERED_CHUNK * WIDTH : (ORDERED_CHUNK + 1) * WIDTH]
            nc.gpsimd.tensor_scalar(
                out=ordered[:].rearrange("p (u m e) -> p u m e", u=2, e=2),
                in0=chunk.rearrange("p (m u e) -> p u m e", u=2, e=2),
                scalar1=one[:],
                scalar2=0.0,
                op0=ALU.mult,
                op1=ALU.add,
            )
            return ordered

        def transpose_rows(rows, unit=-1, ordered=None):
            words = rows[:].bitcast(F32)
            grouped = grouped_pool.tile(
                [P, PASSES * TOKENS * PACK], BF16, name="grouped", align_bytes=256
            )
            grouped_words = grouped[:].bitcast(F32)
            for c in range(CHUNKS):
                bank = psum.tile([P, BANK], F32, name="bank")
                for g in range(PASSES):
                    for u in range(2):
                        if ordered is not None and c == ORDERED_CHUNK:
                            first_word = (u * PASSES + g) * P
                            every_second = ordered[:].bitcast(F32)[:, first_word : first_word + P]
                        else:
                            first_word = c * ROW_WORDS + g * PASS_WORDS
                            every_second = words[:, first_word + u : first_word + PASS_WORDS : 2]
                        nc.tensor.transpose(
                            out=bank[:, (2 * g + u) * P : (2 * g + u + 1) * P],
                            in_=every_second,
                            identity=ident[:],
                        )
                target = grouped_words[:, c * BANK : (c + 1) * BANK].rearrange(
                    "p (g r u) -> p g r u", g=PASSES, u=2
                )
                halves = bank[:].rearrange("p (g u r) -> p g r u", g=PASSES, u=2)
                if unit >= VECTOR_FROM and c == VECTOR_CHUNK:
                    nc.vector.tensor_copy(out=target, in_=halves)
                else:
                    nc.scalar.copy(out=target, in_=halves)
            return grouped

        def quantise_rows(grouped, row_mx, first_chunk=0, end_chunk=CHUNKS):
            codes, scales = row_mx
            cols = slice(first_chunk * CHUNK_COLS, end_chunk * CHUNK_COLS)
            nc.vector.quantize_mx(
                out=codes[:, cols].bitcast(FP8X4),
                scales=scales[:, cols],
                in_=grouped[:, cols.start * PACK : cols.stop * PACK],
            )

        def new_unit_mx():
            codes = unit_mx_pool.tile([P, PASSES * TOKENS], U32, name="unit_codes", align_bytes=256)
            scales = unit_mx_pool.tile([P, PASSES * TOKENS], U8, name="unit_scales", align_bytes=256)
            return codes, scales

        def new_feat():
            return feat_pool.tile([P, TOKENS * PACK], BF16, name="feat", align_bytes=256)

        def new_feat_mx():
            codes = feat_mx_pool.tile([P, TOKENS], U32, name="feat_codes", align_bytes=256)
            scales = feat_mx_pool.tile([P, TOKENS], U8, name="feat_scales", align_bytes=256)
            return codes, scales

        def project_chunk(c, unit_mx, weight_mx, feat):
            codes, scales = unit_mx
            w_codes, w_scales = weight_mx
            bank = psum.tile([P, BANK], F32, name="bank")
            for t in range(PACK):
                for g in range(PASSES):
                    w_cols = slice(t * CHUNK_COLS + g * P, t * CHUNK_COLS + (g + 1) * P)
                    x_cols = slice(c * CHUNK_COLS + g * P, c * CHUNK_COLS + (g + 1) * P)
                    nc.tensor.matmul_mx(
                        out=bank[:, t * P : (t + 1) * P],
                        lhsT=w_codes[:, w_cols].bitcast(FP8X4),
                        lhsT_scale=w_scales[:, w_cols],
                        rhs=codes[:, x_cols].bitcast(FP8X4),
                        rhs_scale=scales[:, x_cols],
                        start=(g == 0),
                        stop=(g == PASSES - 1),
                    )
            nc.scalar.copy(
                out=feat[:, c * BANK : (c + 1) * BANK].rearrange("p (r t) -> p r t", t=PACK),
                in_=bank[:].rearrange("p (t r) -> p r t", t=PACK),
            )

        def quantise_features(feat, feat_mx, first_token=0, end_token=TOKENS):
            codes, scales = feat_mx
            cols = slice(first_token, end_token)
            nc.vector.quantize_mx(
                out=codes[:, cols].bitcast(FP8X4),
                scales=scales[:, cols],
                in_=feat[:, first_token * PACK : end_token * PACK],
            )

        def build_caps():
            for c in range(CHUNKS):
                nc.vector.tensor_scalar(
                    out=caps[:, c * TOKENS : (c + 1) * TOKENS],
                    in0=mask_rows[:, 2 * c * TOKENS : 2 * (c + 1) * TOKENS : 2],
                    scalar1=-2.0 * CAP,
                    scalar2=CAP,
                    op0=ALU.mult,
                    op1=ALU.add,
                )

        def new_softmax(pool=prob_pool, tiles=PAIR):
            prob = pool.tile([P, tiles * TOKENS], F32, name="prob")
            negmax = small.tile([P, tiles], F32, name="negmax")
            rowsum = small.tile([P, tiles], F32, name="rowsum")
            inverse = small.tile([P, tiles], F32, name="inverse")
            return prob, negmax, rowsum, inverse

        def score_tile(tile_no, q_mx, k_mx):
            q_codes, q_scales = q_mx
            k_codes, k_scales = k_mx
            bank = psum.tile([P, BANK], F32, name="bank")
            nc.tensor.matmul_mx(
                out=bank[:],
                lhsT=q_codes[:, tile_no * P : (tile_no + 1) * P].bitcast(FP8X4),
                lhsT_scale=q_scales[:, tile_no * P : (tile_no + 1) * P],
                rhs=k_codes[:].bitcast(FP8X4),
                rhs_scale=k_scales[:],
                start=True,
                stop=True,
            )
            return bank

        def mask_scores(bank, tile_no, i, softmax):
            nc.vector.scalar_tensor_tensor(
                out=softmax[0][:, i * TOKENS : (i + 1) * TOKENS],
                in0=bank[:],
                scalar=SCORE_SCALE,
                in1=caps[:, tile_no * TOKENS : (tile_no + 1) * TOKENS],
                op0=ALU.mult,
                op1=ALU.min,
            )

        def row_maximum(i, softmax):
            prob, negmax = softmax[0], softmax[1]
            nc.vector.tensor_reduce(
                out=negmax[:, i : i + 1],
                in_=prob[:, i * TOKENS : (i + 1) * TOKENS],
                axis=mybir.AxisListType.X,
                op=ALU.max,
                negate=True,
            )

        def exponential(i, softmax):
            prob, negmax, rowsum = softmax[0], softmax[1], softmax[2]
            nc.scalar.activation(
                out=prob[:, i * TOKENS : (i + 1) * TOKENS],
                in_=prob[:, i * TOKENS : (i + 1) * TOKENS],
                func=ACT.Exp,
                bias=negmax[:, i : i + 1],
                scale=1.0,
                accum_out=rowsum[:, i : i + 1],
            )

        def invert(softmax):
            nc.vector.reciprocal(out=softmax[3][:], in_=softmax[2][:])

        def divide(i, softmax, engine):
            prob, inverse = softmax[0], softmax[3]
            engine.tensor_scalar(
                out=prob[:, i * TOKENS : (i + 1) * TOKENS],
                in0=prob[:, i * TOKENS : (i + 1) * TOKENS],
                scalar1=inverse[:, i : i + 1],
                scalar2=0.0,
                op0=ALU.mult,
                op1=ALU.add,
            )

        def store(b, tile_no, i, softmax):
            nc.sync.dma_start(
                out=out[b, tile_no * P : (tile_no + 1) * P, :],
                in_=softmax[0][:, i * TOKENS : (i + 1) * TOKENS],
            )

        def score_pair(pair):
            b, first = divmod(pair * PAIR, CHUNKS)
            softmax = new_softmax()
            for i in range(PAIR):
                bank = score_tile(first + i, feat_mx[2 * b + 1], feat_mx[2 * b])
                mask_scores(bank, first + i, i, softmax)
            return softmax

        def find_maxima(softmax):
            nc.vector.tensor_reduce(
                out=softmax[1][:],
                in_=softmax[0][:].rearrange("p (i k) -> p i k", i=PAIR),
                axis=mybir.AxisListType.X,
                op=ALU.max,
                negate=True,
            )

        def exponentials(softmax):
            for i in range(PAIR):
                exponential(i, softmax)

        def normalise_and_store(pair, softmax):
            b, first = divmod(pair * PAIR, CHUNKS)
            invert(softmax)
            for i in range(PAIR):
                divide(i, softmax, nc.gpsimd)
                store(b, first + i, i, softmax)

        ident = const.tile([P, P], F32, name="ident", align_bytes=256)
        make_identity(nc, ident[:])
        warm = const.tile([P, 1], F32, name="warm")
        nc.vector.memset(warm[:], 0.0)
        nc.scalar.activation(out=warm[:], in_=warm[:], func=ACT.Exp)

        rows = {}
        entangle_rows = load_weight(entangle_params)
        rows[0] = load_unit(0)
        rotation_rows = load_weight(rotation_params)
        for unit in range(1, PREFETCH):
            rows[unit] = load_unit(unit)
        mask_rows = const.tile([P, CHUNKS * 2 * TOKENS], I32, name="mask_rows")
        mask_words = mask.bitcast(I32)
        for c in range(CHUNKS):
            nc.sync.dma_start(
                out=mask_rows[:, 2 * c * TOKENS : 2 * (c + 1) * TOKENS],
                in_=mask_words[c * P : (c + 1) * P, :],
            )
        caps = const.tile([P, CHUNKS * TOKENS], F32, name="caps")

        weight_mx = []
        unit_mx = {}
        for name in ("entangle", "rotation"):
            weight_mx.append(
                (
                    const.tile([P, PASSES * FEATURES], U32, name=name + "_codes", align_bytes=256),
                    const.tile([P, PASSES * FEATURES], U8, name=name + "_scales", align_bytes=256),
                )
            )
        quantise_rows(transpose_rows(entangle_rows), weight_mx[0])
        unit_mx[0] = new_unit_mx()
        quantise_rows(transpose_rows(rows[0], 0), unit_mx[0])
        quantise_rows(transpose_rows(rotation_rows), weight_mx[1])

        feat_mx = {}
        softmax = {}
        ordered = ordered_next = None
        for step in range(UNITS):
            ahead = step + PREFETCH
            following = step + 1
            scoring = step - 2
            raising = step - 3
            dividing = step - 4
            if ahead < UNITS:
                rows[ahead] = load_unit(ahead)
            if following < UNITS:
                grouped = transpose_rows(rows[following], following, ordered)
            if scoring == 0:
                build_caps()
            if 0 <= scoring < PAIRS - 3:
                softmax[scoring] = score_pair(scoring)
            if following < UNITS:
                unit_mx[following] = new_unit_mx()
                quantise_rows(grouped, unit_mx[following])
            if 0 <= dividing < PAIRS - 5:
                normalise_and_store(dividing, softmax[dividing])
            feat = new_feat()
            for c in range(CHUNKS):
                project_chunk(c, unit_mx[step], weight_mx[step % 2], feat)
            if 0 <= scoring < PAIRS - 3:
                find_maxima(softmax[scoring])
            if raising >= 0:
                exponentials(softmax[raising])
            if step == LAST - 1:
                softmax[scoring + 1] = score_pair(scoring + 1)
            feat_mx[step] = new_feat_mx()
            if step < LAST:
                quantise_features(feat, feat_mx[step])
            ordered = ordered_next
            ordered_next = order_words(rows[following + 2]) if 2 <= following + 2 < UNITS else None
            if step == LAST - 1:
                find_maxima(softmax[scoring + 1])

        per_half = CHUNKS // 2
        before = softmax[PAIRS - 3]
        tiles = [new_softmax(last_prob_pool, 1) for c in range(CHUNKS)]
        quantise_features(feat, feat_mx[LAST], 0, per_half * P)
        quantise_features(feat, feat_mx[LAST], per_half * P, TOKENS)
        banks = [score_tile(c, feat_mx[LAST], feat_mx[LAST - 1]) for c in range(CHUNKS)]
        exponentials(before)
        normalise_and_store(PAIRS - 5, softmax[PAIRS - 5])
        mask_scores(banks[0], 0, 0, tiles[0])
        normalise_and_store(PAIRS - 4, softmax[PAIRS - 4])
        for c in range(CHUNKS):
            if c + 1 < CHUNKS:
                mask_scores(banks[c + 1], c + 1, 0, tiles[c + 1])
            row_maximum(0, tiles[c])
            exponential(0, tiles[c])
            if c == 0:
                normalise_and_store(PAIRS - 3, before)
            else:
                invert(tiles[c - 1])
                divide(0, tiles[c - 1], nc.gpsimd)
                store(BATCH - 1, c - 1, 0, tiles[c - 1])
        invert(tiles[CHUNKS - 1])
        divide(0, tiles[CHUNKS - 1], nc.vector)
        store(BATCH - 1, CHUNKS - 1, 0, tiles[CHUNKS - 1])
